import numpy as np
import ml_dtypes


def mxq(x, axis, fmt="e4m3"):
    dtype, down = {"e4m3": (ml_dtypes.float8_e4m3fn, 7), "e5m2": (ml_dtypes.float8_e5m2, 14)}[fmt]
    v = np.moveaxis(np.asarray(x, np.float32).astype(ml_dtypes.bfloat16).astype(np.float64), axis, -1)
    blocks = v.reshape(v.shape[:-1] + (-1, 32))
    amax = np.abs(blocks).max(-1, keepdims=True)
    byte = np.maximum(np.where(amax > 0, np.frexp(amax)[1] - 1 + 127, 0) - down, 1)
    scale = np.exp2(byte - 127.0)
    codes = (blocks / scale).astype(np.float32).astype(dtype).astype(np.float64)
    return np.moveaxis((codes * scale).reshape(v.shape), -1, axis)


WIDE = False


def mx_kscale(k):
    if not WIDE:
        return np.ones(k)
    levels = np.array([10, -10, 5, -5, 0])
    a = np.random.permutation(np.resize(levels, k // 512 * 4)).reshape(k // 512, 4)
    idx = np.arange(k)
    return np.exp2(a[idx // 512, idx % 128 // 32])


BF16 = ml_dtypes.bfloat16


def bf(x):
    return np.asarray(x, np.float32).astype(BF16)


def f64(x):
    return np.asarray(x).astype(np.float64)


B, S, I, O, NB, G = 2, 256, 1024, 1024, 5, 1


def setup_inputs():
    s = mx_kscale(I)
    return {"x": bf(np.random.standard_normal((B, S, I)) * s),
            "basis_coeffs": bf(np.random.standard_normal((I, O // G, NB)) / np.sqrt(I)),
            "linear_w": bf(np.random.standard_normal((O, I)) / np.sqrt(I) / s),
            "pathway_balance": bf(0.5 + 0.1 * np.random.standard_normal(2))}


def reference(x, basis_coeffs, linear_w, pathway_balance):
    x = f64(x)
    pathway_balance = f64(pathway_balance)
    shape = x.shape[:-1]
    x_flat = x.reshape(-1, I)
    x_norm = np.tanh(x_flat)
    powers = np.arange(NB, dtype=np.float64)
    basis = x_norm[..., None] ** powers
    bq = mxq(basis, 1, "e4m3").transpose(2, 0, 1)
    cq = mxq(f64(basis_coeffs), 0, "e4m3").transpose(2, 0, 1)
    nonlinear_out = (bq @ cq).sum(0)
    if G > 1:
        nonlinear_out = np.tile(nonlinear_out, (1, G))
    linear_out = mxq(x_flat, 1, "e4m3") @ mxq(f64(linear_w), 1, "e4m3").T
    y = pathway_balance[0] * nonlinear_out + pathway_balance[1] * linear_out
    return y.reshape(*shape, O)

@@ -1,0 +1,210 @@
+from contextlib import ExitStack
+
+import concourse.mybir as mybir
+from concourse.masks import make_identity
+
+F32 = mybir.dt.float32
+BF16 = mybir.dt.bfloat16
+U32 = mybir.dt.uint32
+U8 = mybir.dt.uint8
+FP8X4 = mybir.dt.float8_e4m3fn_x4
+AF = mybir.ActivationFunctionType
+ALU = mybir.AluOpType
+
+P = 128
+R = 512
+I = 1024
+O = 1024
+NB = 5
+MT = R // P
+G = I // 512
+OC = 256
+NCH = O // OC
+FLOPS = 2 * R * I * O * (NB + 1)
+
+SCALAR_PIECE = ("B", "B", "A", "B", "B", "A", "B", "B")
+CRAW_BUFS = 5
+
+
+def tile_kolmogorovarnoldlinear_kernel(tc, x, basis_coeffs, linear_w, pathway_balance, out):
+    nc = tc.nc
+    xf = x.flatten_outer_dims()
+    of = out.flatten_outer_dims()
+    with ExitStack() as ctx:
+        keep = ctx.enter_context(tc.tile_pool(name="keep", bufs=1))
+        work = ctx.enter_context(tc.tile_pool(name="work", bufs=2))
+        psum = ctx.enter_context(tc.psum_pool(name="psum", bufs=8))
+
+        x_sb = keep.tile([P, MT, I], BF16)
+        for m in range(MT):
+            nc.sync.dma_start(out=x_sb[:, m, :], in_=xf[m * P:(m + 1) * P, :])
+        pb_bf = keep.tile([P, 2], BF16)
+        nc.scalar.dma_start(out=pb_bf[:], in_=pathway_balance.partition_broadcast(P))
+
+        halves = [(c, g) for c in range(NCH) for g in range(G)]
+        craw = {}
+
+        def load_half(h):
+            c, g = halves[h]
+            t = work.tile([P, 4, OC * NB], BF16, name="craw%d" % h, tag="craw", bufs=CRAW_BUFS)
+            nc.sync.dma_start(
+                out=t[:],
+                in_=basis_coeffs[512 * g:512 * g + 512, OC * c:OC * c + OC, :].rearrange("(p j) o n -> p j (o n)", j=4),
+            )
+            craw[h] = t
+
+        load_half(0)
+        load_half(1)
+        w_sb = keep.tile([P, O // P, I], BF16)
+        wv = linear_w.rearrange("(a p) i -> p a i", p=P)
+        for q in range(2):
+            nc.sync.dma_start(out=w_sb[:, 4 * q:4 * q + 4, :], in_=wv[:, 4 * q:4 * q + 4, :])
+        for h in range(2, CRAW_BUFS):
+            load_half(h)
+
+        ident = keep.tile([P, P], F32)
+        make_identity(nc, ident[:])
+        ones = keep.tile([P, 512], BF16, align_bytes=64)
+        nc.vector.memset(ones[:], 1.0)
+        oneq = keep.tile([P, P], U32, align_bytes=64)
+        ones_s = keep.tile([P, P], U8, align_bytes=64)
+        nc.vector.quantize_mx(out=oneq[:].bitcast(FP8X4), scales=ones_s[:], in_=ones[:])
+        pb32 = keep.tile([P, 2], F32)
+        nc.vector.tensor_copy(out=pb32[:], in_=pb_bf[:])
+
+        xw = x_sb[:].bitcast(F32)
+        xq = keep.tile([P, MT, 256], U32, align_bytes=64)
+        xs = keep.tile([P, MT, 256], U8, align_bytes=64)
+        aq = keep.tile([P, MT, 1024], U32, align_bytes=64)
+        as_ = keep.tile([P, MT, 1024], U8, align_bytes=64)
+        for m in range(MT):
+            xt = psum.tile([P, 512], F32, name="xt%d" % m, tag="bank")
+            for u in range(2):
+                for g in range(G):
+                    k = 2 * u + g
+                    nc.tensor.transpose(
+                        out=xt[:, k * P:(k + 1) * P],
+                        in_=xw[:, m, 256 * g + u:256 * g + 256:2],
+                        identity=ident[:],
+                    )
+            t32 = work.tile([P, 1024], F32, tag="t32")
+            nc.scalar.activation(
+                out=t32[:].rearrange("p (q u e) -> p q u e", u=2, e=2),
+                in_=xt[:].bitcast(BF16).rearrange("p (u q e) -> p q u e", u=2, e=2),
+                func=AF.Tanh,
+            )
+            xg = work.tile([P, 1024], BF16, tag="xg", align_bytes=64)
+            nc.scalar.copy(
+                out=xg[:].bitcast(F32).rearrange("p (q u) -> p q u", u=2),
+                in_=xt[:].rearrange("p (u q) -> p q u", u=2),
+            )
+            s32 = work.tile([P, 1024], F32, tag="s32")
+            nc.scalar.activation(out=s32[:], in_=t32[:], func=AF.Square)
+            ain = work.tile([P, 4, 1024], BF16, tag="ain", align_bytes=64)
+            nc.vector.tensor_copy(out=ain[:, 0, :], in_=t32[:])
+            nc.scalar.activation(out=ain[:, 3, :], in_=s32[:], func=AF.Square)
+            nc.vector.tensor_copy(out=ain[:, 1, :], in_=s32[:])
+            nc.vector.tensor_tensor(out=ain[:, 2, :], in0=s32[:], in1=t32[:], op=ALU.mult)
+            nc.vector.quantize_mx(out=xq[:, m, :].bitcast(FP8X4), scales=xs[:, m, :], in_=xg[:])
+            nc.vector.quantize_mx(
+                out=aq[:, m, :].bitcast(FP8X4), scales=as_[:, m, :], in_=ain[:].rearrange("p a c -> p (a c)")
+            )
+
+        ww = w_sb[:].bitcast(F32)
+        wq = keep.tile([P, G, O], U32, align_bytes=64)
+        ws = keep.tile([P, G, O], U8, align_bytes=64)
+        for g in range(G):
+            for hq in range(2):
+                wg = work.tile([P, 2048], BF16, tag="wg", align_bytes=64)
+                wg32 = wg[:].bitcast(F32).rearrange("p (o u) -> p o u", u=2)
+                for pair in range(2):
+                    wt = psum.tile([P, 512], F32, name="wt%d%d%d" % (g, hq, pair), tag="bank")
+                    for a2 in range(2):
+                        a = 4 * hq + 2 * pair + a2
+                        for u in range(2):
+                            nc.tensor.transpose(
+                                out=wt[:, u * 256 + a2 * P:u * 256 + (a2 + 1) * P],
+                                in_=ww[:, a, 256 * g + u:256 * g + 256:2],
+                                identity=ident[:],
+                            )
+                    nc.scalar.copy(
+                        out=wg32[:, 256 * pair:256 * pair + 256, :],
+                        in_=wt[:].rearrange("p (u o) -> p o u", u=2),
+                    )
+                nc.vector.quantize_mx(
+                    out=wq[:, g, 512 * hq:512 * hq + 512].bitcast(FP8X4),
+                    scales=ws[:, g, 512 * hq:512 * hq + 512],
+                    in_=wg[:],
+                )
+
+        y = keep.tile([P, MT, O], F32)
+        for m in range(MT):
+            for h in range(2):
+                lacc = psum.tile([P, 512], F32, name="lacc%d%d" % (m, h), tag="bank")
+                for g in range(G):
+                    nc.tensor.matmul_mx(
+                        out=lacc[:],
+                        lhsT=xq[:, m, g * P:(g + 1) * P].bitcast(FP8X4),
+                        lhsT_scale=xs[:, m, g * P:(g + 1) * P],
+                        rhs=wq[:, g, 512 * h:512 * h + 512].bitcast(FP8X4),
+                        rhs_scale=ws[:, g, 512 * h:512 * h + 512],
+                        start=(g == 0),
+                        stop=(g == G - 1),
+                    )
+                nc.scalar.activation(
+                    out=y[:, m, 512 * h:512 * h + 512], in_=lacc[:], func=AF.Copy, scale=pb32[:, 1:2]
+                )
+
+        ov = of.rearrange("(m p) o -> p m o", p=P)
+        for c in range(NCH):
+            nacc = [psum.tile([P, 512], F32, name="nacc%d_%d" % (c, m), tag="bank") for m in range(MT)]
+            for g in range(G):
+                h = c * G + g
+                src = craw[h][:].rearrange("p j (o n) -> p o n j", n=NB)
+                cga = work.tile([P, 3, OC, 4], BF16, tag="cga", bufs=3, align_bytes=64)
+                cgb = work.tile([P, 2, OC, 4], BF16, tag="cgb", bufs=3, align_bytes=64)
+                for piece, cg, lo, hi in (("A", cga, 0, 3), ("B", cgb, 3, 5)):
+                    dst = cg[:].rearrange("p n o j -> p o n j")
+                    if SCALAR_PIECE[h] == piece:
+                        nc.scalar.copy(out=dst, in_=src[:, :, lo:hi, :])
+                    else:
+                        nc.vector.tensor_copy(out=dst, in_=src[:, :, lo:hi, :])
+                if h + CRAW_BUFS < len(halves):
+                    load_half(h + CRAW_BUFS)
+                cq = work.tile([P, NB, OC], U32, tag="cq", bufs=4, align_bytes=64)
+                cs = work.tile([P, NB, OC], U8, tag="cs", bufs=4, align_bytes=64)
+                for cg, base, lo, hi in ((cga, 0, 0, 2), (cga, 0, 2, 3), (cgb, 3, 3, 5)):
+                    nc.vector.quantize_mx(
+                        out=cq[:, lo:hi, :].rearrange("p n o -> p (n o)").bitcast(FP8X4),
+                        scales=cs[:, lo:hi, :].rearrange("p n o -> p (n o)"),
+                        in_=cg[:, lo - base:hi - base, :, :].rearrange("p n o j -> p (n o j)"),
+                    )
+                for n in range(NB):
+                    for m in range(MT):
+                        if n == 0:
+                            lhsT, lsc = oneq[:], ones_s[:]
+                        else:
+                            k = (n - 1) * G + g
+                            lhsT, lsc = aq[:, m, k * P:(k + 1) * P], as_[:, m, k * P:(k + 1) * P]
+                        nc.tensor.matmul_mx(
+                            out=nacc[m][:, 0:OC],
+                            lhsT=lhsT.bitcast(FP8X4),
+                            lhsT_scale=lsc,
+                            rhs=cq[:, n, :].bitcast(FP8X4),
+                            rhs_scale=cs[:, n, :],
+                            start=(g == 0 and n == 0),
+                            stop=(g == G - 1 and n == NB - 1),
+                        )
+            for m in range(MT):
+                nc.vector.scalar_tensor_tensor(
+                    out=y[:, m, OC * c:OC * c + OC],
+                    in0=nacc[m][:, 0:OC],
+                    scalar=pb32[:, 0:1],
+                    in1=y[:, m, OC * c:OC * c + OC],
+                    op0=ALU.mult,
+                    op1=ALU.add,
+                )
+                if c == NCH - 1:
+                    nc.sync.dma_start(out=ov[:, m, OC * c:OC * c + OC], in_=y[:, m, OC * c:OC * c + OC])
+            if c < NCH - 1:
+                nc.sync.dma_start(out=ov[:, :, OC * c:OC * c + OC], in_=y[:, :, OC * c:OC * c + OC])

@@ -20,20 +20,24 @@ MT = R // P
 G = I // 512
 OC = 256
 NCH = O // OC
+NH = NCH * G
 FLOPS = 2 * R * I * O * (NB + 1)
 
-SCALAR_PIECE = ("B", "B", "A", "B", "B", "A", "B", "B")
 CRAW_BUFS = 5
+FIRST_SCALAR_HALF = 2
+FORM = 1
 
 
 def tile_kolmogorovarnoldlinear_kernel(tc, x, basis_coeffs, linear_w, pathway_balance, out):
     nc = tc.nc
     xf = x.flatten_outer_dims()
     of = out.flatten_outer_dims()
+    ov = of.rearrange("(m p) o -> p m o", p=P)
     with ExitStack() as ctx:
         keep = ctx.enter_context(tc.tile_pool(name="keep", bufs=1))
         work = ctx.enter_context(tc.tile_pool(name="work", bufs=2))
         psum = ctx.enter_context(tc.psum_pool(name="psum", bufs=8))
+        ctx.enter_context(tc.manual_schedule())
 
         x_sb = keep.tile([P, MT, I], BF16)
         for m in range(MT):
@@ -41,11 +45,10 @@ def tile_kolmogorovarnoldlinear_kernel(tc, x, basis_coeffs, linear_w, pathway_ba
         pb_bf = keep.tile([P, 2], BF16)
         nc.scalar.dma_start(out=pb_bf[:], in_=pathway_balance.partition_broadcast(P))
 
-        halves = [(c, g) for c in range(NCH) for g in range(G)]
         craw = {}
 
         def load_half(h):
-            c, g = halves[h]
+            c, g = divmod(h, G)
             t = work.tile([P, 4, OC * NB], BF16, name="craw%d" % h, tag="craw", bufs=CRAW_BUFS)
             nc.sync.dma_start(
                 out=t[:],
@@ -73,132 +76,138 @@ def tile_kolmogorovarnoldlinear_kernel(tc, x, basis_coeffs, linear_w, pathway_ba
         nc.vector.tensor_copy(out=pb32[:], in_=pb_bf[:])
 
         xw = x_sb[:].bitcast(F32)
+        ww = w_sb[:].bitcast(F32)
         xq = keep.tile([P, MT, 256], U32, align_bytes=64)
         xs = keep.tile([P, MT, 256], U8, align_bytes=64)
         aq = keep.tile([P, MT, 1024], U32, align_bytes=64)
         as_ = keep.tile([P, MT, 1024], U8, align_bytes=64)
-        for m in range(MT):
-            xt = psum.tile([P, 512], F32, name="xt%d" % m, tag="bank")
+        wq = keep.tile([P, G, O], U32, align_bytes=64)
+        ws = keep.tile([P, G, O], U8, align_bytes=64)
+        y = keep.tile([P, MT, O], F32)
+
+        xt = {}
+        wt = {}
+
+        def transpose_x(m):
+            xt[m] = psum.tile([P, 512], F32, name="xt%d" % m, tag="bank")
             for u in range(2):
                 for g in range(G):
                     k = 2 * u + g
                     nc.tensor.transpose(
-                        out=xt[:, k * P:(k + 1) * P],
+                        out=xt[m][:, k * P:(k + 1) * P],
                         in_=xw[:, m, 256 * g + u:256 * g + 256:2],
                         identity=ident[:],
                     )
-            t32 = work.tile([P, 1024], F32, tag="t32")
-            nc.scalar.activation(
-                out=t32[:].rearrange("p (q u e) -> p q u e", u=2, e=2),
-                in_=xt[:].bitcast(BF16).rearrange("p (u q e) -> p q u e", u=2, e=2),
-                func=AF.Tanh,
-            )
+
+        def transpose_w(i):
+            hq, g, pair = i // 4, (i // 2) % 2, i % 2
+            wt[i] = psum.tile([P, 512], F32, name="wt%d" % i, tag="bank")
+            for a2 in range(2):
+                a = 4 * hq + 2 * pair + a2
+                for u in range(2):
+                    nc.tensor.transpose(
+                        out=wt[i][:, u * 256 + a2 * P:u * 256 + (a2 + 1) * P],
+                        in_=ww[:, a, 256 * g + u:256 * g + 256:2],
+                        identity=ident[:],
+                    )
+
+        for m in range(MT):
+            transpose_x(m)
+        for i in range(4):
+            transpose_w(i)
+
+        for m in range(MT):
             xg = work.tile([P, 1024], BF16, tag="xg", align_bytes=64)
             nc.scalar.copy(
                 out=xg[:].bitcast(F32).rearrange("p (q u) -> p q u", u=2),
-                in_=xt[:].rearrange("p (u q) -> p q u", u=2),
+                in_=xt[m][:].rearrange("p (u q) -> p q u", u=2),
+            )
+            t32 = work.tile([P, 1024], F32, tag="t32")
+            nc.scalar.activation(
+                out=t32[:].rearrange("p (q u e) -> p q u e", u=2, e=2),
+                in_=xt[m][:].bitcast(BF16).rearrange("p (u q e) -> p q u e", u=2, e=2),
+                func=AF.Tanh,
             )
             s32 = work.tile([P, 1024], F32, tag="s32")
             nc.scalar.activation(out=s32[:], in_=t32[:], func=AF.Square)
             ain = work.tile([P, 4, 1024], BF16, tag="ain", align_bytes=64)
-            nc.vector.tensor_copy(out=ain[:, 0, :], in_=t32[:])
             nc.scalar.activation(out=ain[:, 3, :], in_=s32[:], func=AF.Square)
+            nc.vector.quantize_mx(out=xq[:, m, :].bitcast(FP8X4), scales=xs[:, m, :], in_=xg[:])
+            nc.vector.tensor_copy(out=ain[:, 0, :], in_=t32[:])
             nc.vector.tensor_copy(out=ain[:, 1, :], in_=s32[:])
             nc.vector.tensor_tensor(out=ain[:, 2, :], in0=s32[:], in1=t32[:], op=ALU.mult)
-            nc.vector.quantize_mx(out=xq[:, m, :].bitcast(FP8X4), scales=xs[:, m, :], in_=xg[:])
             nc.vector.quantize_mx(
                 out=aq[:, m, :].bitcast(FP8X4), scales=as_[:, m, :], in_=ain[:].rearrange("p a c -> p (a c)")
             )
+            transpose_w(4 + m)
 
-        ww = w_sb[:].bitcast(F32)
-        wq = keep.tile([P, G, O], U32, align_bytes=64)
-        ws = keep.tile([P, G, O], U8, align_bytes=64)
-        for g in range(G):
-            for hq in range(2):
-                wg = work.tile([P, 2048], BF16, tag="wg", align_bytes=64)
-                wg32 = wg[:].bitcast(F32).rearrange("p (o u) -> p o u", u=2)
-                for pair in range(2):
-                    wt = psum.tile([P, 512], F32, name="wt%d%d%d" % (g, hq, pair), tag="bank")
-                    for a2 in range(2):
-                        a = 4 * hq + 2 * pair + a2
-                        for u in range(2):
-                            nc.tensor.transpose(
-                                out=wt[:, u * 256 + a2 * P:u * 256 + (a2 + 1) * P],
-                                in_=ww[:, a, 256 * g + u:256 * g + 256:2],
-                                identity=ident[:],
-                            )
-                    nc.scalar.copy(
-                        out=wg32[:, 256 * pair:256 * pair + 256, :],
-                        in_=wt[:].rearrange("p (u o) -> p o u", u=2),
-                    )
-                nc.vector.quantize_mx(
-                    out=wq[:, g, 512 * hq:512 * hq + 512].bitcast(FP8X4),
-                    scales=ws[:, g, 512 * hq:512 * hq + 512],
-                    in_=wg[:],
-                )
+        cga = {}
+        cgb = {}
+        cq = {}
+        cs = {}
 
-        y = keep.tile([P, MT, O], F32)
-        for m in range(MT):
-            for h in range(2):
-                lacc = psum.tile([P, 512], F32, name="lacc%d%d" % (m, h), tag="bank")
-                for g in range(G):
-                    nc.tensor.matmul_mx(
-                        out=lacc[:],
-                        lhsT=xq[:, m, g * P:(g + 1) * P].bitcast(FP8X4),
-                        lhsT_scale=xs[:, m, g * P:(g + 1) * P],
-                        rhs=wq[:, g, 512 * h:512 * h + 512].bitcast(FP8X4),
-                        rhs_scale=ws[:, g, 512 * h:512 * h + 512],
-                        start=(g == 0),
-                        stop=(g == G - 1),
-                    )
-                nc.scalar.activation(
-                    out=y[:, m, 512 * h:512 * h + 512], in_=lacc[:], func=AF.Copy, scale=pb32[:, 1:2]
-                )
+        def regroup(eng, dst_tile, h, lo, hi, base):
+            if FORM == 1:
+                src = craw[h][:].rearrange("p j (o n) -> p o n j", n=NB)[:, :, lo:hi, :]
+                dst = dst_tile[:, lo - base:hi - base, :, :].rearrange("p n o j -> p o n j")
+            else:
+                src = craw[h][:].rearrange("p j (o n) -> p o j n", n=NB)[:, :, :, lo:hi]
+                dst = dst_tile[:, lo - base:hi - base, :, :].rearrange("p n o j -> p o j n")
+            if eng == "scalar":
+                nc.scalar.copy(out=dst, in_=src)
+            else:
+                nc.vector.tensor_copy(out=dst, in_=src)
 
-        ov = of.rearrange("(m p) o -> p m o", p=P)
-        for c in range(NCH):
-            nacc = [psum.tile([P, 512], F32, name="nacc%d_%d" % (c, m), tag="bank") for m in range(MT)]
-            for g in range(G):
-                h = c * G + g
-                src = craw[h][:].rearrange("p j (o n) -> p o n j", n=NB)
-                cga = work.tile([P, 3, OC, 4], BF16, tag="cga", bufs=3, align_bytes=64)
-                cgb = work.tile([P, 2, OC, 4], BF16, tag="cgb", bufs=3, align_bytes=64)
-                for piece, cg, lo, hi in (("A", cga, 0, 3), ("B", cgb, 3, 5)):
-                    dst = cg[:].rearrange("p n o j -> p o n j")
-                    if SCALAR_PIECE[h] == piece:
-                        nc.scalar.copy(out=dst, in_=src[:, :, lo:hi, :])
+        def regroup_a(h, eng):
+            cga[h] = work.tile([P, 3, OC, 4], BF16, name="cga%d" % h, tag="cga", bufs=4, align_bytes=64)
+            if eng == "scalar":
+                regroup(eng, cga[h], h, 0, 3, 0)
+            else:
+                regroup(eng, cga[h], h, 0, 2, 0)
+                regroup(eng, cga[h], h, 2, 3, 0)
+
+        def regroup_b(h):
+            cgb[h] = work.tile([P, 2, OC, 4], BF16, name="cgb%d" % h, tag="cgb", bufs=2, align_bytes=64)
+            regroup("vector", cgb[h], h, 3, 5, 3)
+
+        def vector_regroups(h):
+            if h < FIRST_SCALAR_HALF:
+                regroup_a(h, "vector")
+            regroup_b(h)
+
+        def quantise(h, cg, base, lo, hi):
+            nc.vector.quantize_mx(
+                out=cq[h][:, lo:hi, :].rearrange("p n o -> p (n o)").bitcast(FP8X4),
+                scales=cs[h][:, lo:hi, :].rearrange("p n o -> p (n o)"),
+                in_=cg[:, lo - base:hi - base, :, :].rearrange("p n o j -> p (n o j)"),
+            )
+
+        nacc = {}
+
+        def passes(h, powers, first, last):
+            c, g = divmod(h, G)
+            for n in powers:
+                for m in range(MT):
+                    if n == 0:
+                        lhsT, lsc = oneq[:], ones_s[:]
                     else:
-                        nc.vector.tensor_copy(out=dst, in_=src[:, :, lo:hi, :])
-                if h + CRAW_BUFS < len(halves):
-                    load_half(h + CRAW_BUFS)
-                cq = work.tile([P, NB, OC], U32, tag="cq", bufs=4, align_bytes=64)
-                cs = work.tile([P, NB, OC], U8, tag="cs", bufs=4, align_bytes=64)
-                for cg, base, lo, hi in ((cga, 0, 0, 2), (cga, 0, 2, 3), (cgb, 3, 3, 5)):
-                    nc.vector.quantize_mx(
-                        out=cq[:, lo:hi, :].rearrange("p n o -> p (n o)").bitcast(FP8X4),
-                        scales=cs[:, lo:hi, :].rearrange("p n o -> p (n o)"),
-                        in_=cg[:, lo - base:hi - base, :, :].rearrange("p n o j -> p (n o j)"),
+                        k = (n - 1) * G + g
+                        lhsT, lsc = aq[:, m, k * P:(k + 1) * P], as_[:, m, k * P:(k + 1) * P]
+                    nc.tensor.matmul_mx(
+                        out=nacc[c][m][:, 0:OC],
+                        lhsT=lhsT.bitcast(FP8X4),
+                        lhsT_scale=lsc,
+                        rhs=cq[h][:, n, :].bitcast(FP8X4),
+                        rhs_scale=cs[h][:, n, :],
+                        start=(first and n == powers[0]),
+                        stop=(last and n == powers[-1]),
                     )
-                for n in range(NB):
-                    for m in range(MT):
-                        if n == 0:
-                            lhsT, lsc = oneq[:], ones_s[:]
-                        else:
-                            k = (n - 1) * G + g
-                            lhsT, lsc = aq[:, m, k * P:(k + 1) * P], as_[:, m, k * P:(k + 1) * P]
-                        nc.tensor.matmul_mx(
-                            out=nacc[m][:, 0:OC],
-                            lhsT=lhsT.bitcast(FP8X4),
-                            lhsT_scale=lsc,
-                            rhs=cq[:, n, :].bitcast(FP8X4),
-                            rhs_scale=cs[:, n, :],
-                            start=(g == 0 and n == 0),
-                            stop=(g == G - 1 and n == NB - 1),
-                        )
+
+        def finish(c):
             for m in range(MT):
                 nc.vector.scalar_tensor_tensor(
                     out=y[:, m, OC * c:OC * c + OC],
-                    in0=nacc[m][:, 0:OC],
+                    in0=nacc[c][m][:, 0:OC],
                     scalar=pb32[:, 0:1],
                     in1=y[:, m, OC * c:OC * c + OC],
                     op0=ALU.mult,
@@ -208,3 +217,71 @@ def tile_kolmogorovarnoldlinear_kernel(tc, x, basis_coeffs, linear_w, pathway_ba
                     nc.sync.dma_start(out=ov[:, m, OC * c:OC * c + OC], in_=y[:, m, OC * c:OC * c + OC])
             if c < NCH - 1:
                 nc.sync.dma_start(out=ov[:, :, OC * c:OC * c + OC], in_=y[:, :, OC * c:OC * c + OC])
+
+        wg = {}
+        for i in range(8):
+            if i % 2 == 0:
+                wg[i // 2] = work.tile([P, 2048], BF16, name="wg%d" % (i // 2), tag="wg", bufs=2, align_bytes=64)
+            wg32 = wg[i // 2][:].bitcast(F32).rearrange("p (o u) -> p o u", u=2)
+            pair = i % 2
+            nc.scalar.copy(
+                out=wg32[:, 256 * pair:256 * pair + 256, :],
+                in_=wt[i][:].rearrange("p (u o) -> p o u", u=2),
+            )
+            if i == 3:
+                vector_regroups(0)
+                load_half(CRAW_BUFS)
+            if i % 2 == 1:
+                hq, g = i // 4, (i // 2) % 2
+                nc.vector.quantize_mx(
+                    out=wq[:, g, 512 * hq:512 * hq + 512].bitcast(FP8X4),
+                    scales=ws[:, g, 512 * hq:512 * hq + 512],
+                    in_=wg[i // 2][:],
+                )
+        regroup_a(FIRST_SCALAR_HALF, "scalar")
+        for m in range(MT):
+            for hf in range(2):
+                lacc = psum.tile([P, 512], F32, name="lacc%d%d" % (m, hf), tag="bank")
+                for g in range(G):
+                    nc.tensor.matmul_mx(
+                        out=lacc[:],
+                        lhsT=xq[:, m, g * P:(g + 1) * P].bitcast(FP8X4),
+                        lhsT_scale=xs[:, m, g * P:(g + 1) * P],
+                        rhs=wq[:, g, 512 * hf:512 * hf + 512].bitcast(FP8X4),
+                        rhs_scale=ws[:, g, 512 * hf:512 * hf + 512],
+                        start=(g == 0),
+                        stop=(g == G - 1),
+                    )
+                nc.scalar.activation(
+                    out=y[:, m, 512 * hf:512 * hf + 512], in_=lacc[:], func=AF.Copy, scale=pb32[:, 1:2]
+                )
+
+        for h in range(NH + 2):
+            if h + 1 < NH:
+                vector_regroups(h + 1)
+                if h + 1 < FIRST_SCALAR_HALF and h + 1 + CRAW_BUFS < NH:
+                    load_half(h + 1 + CRAW_BUFS)
+            if h < NH:
+                c, g = divmod(h, G)
+                if g == 0:
+                    nacc[c] = [psum.tile([P, 512], F32, name="nacc%d_%d" % (c, m), tag="bank") for m in range(MT)]
+                cq[h] = work.tile([P, NB, OC], U32, name="cq%d" % h, tag="cq", bufs=4, align_bytes=64)
+                cs[h] = work.tile([P, NB, OC], U8, name="cs%d" % h, tag="cs", bufs=4, align_bytes=64)
+                if h < FIRST_SCALAR_HALF:
+                    quantise(h, cga[h], 0, 0, 2)
+                    quantise(h, cga[h], 0, 2, 3)
+                    quantise(h, cgb[h], 3, 3, 5)
+                    passes(h, (0, 1, 2), g == 0, False)
+                    passes(h, (3, 4), False, g == G - 1)
+                else:
+                    quantise(h, cgb[h], 3, 3, 5)
+                    quantise(h, cga[h], 0, 0, 2)
+                    quantise(h, cga[h], 0, 2, 3)
+                    passes(h, (3, 4), g == 0, False)
+                    passes(h, (0, 1, 2), False, g == G - 1)
+                    if h + CRAW_BUFS < NH:
+                        load_half(h + CRAW_BUFS)
+                if FIRST_SCALAR_HALF < h + 3 < NH:
+                    regroup_a(h + 3, "scalar")
+            if h >= 3 and h % 2 == 1:
+                finish((h - 3) // 2)

@@ -25,7 +25,7 @@ FLOPS = 2 * R * I * O * (NB + 1)
 
 CRAW_BUFS = 5
 FIRST_SCALAR_HALF = 2
-FORM = 1
+FORM = 2
 
 
 def tile_kolmogorovarnoldlinear_kernel(tc, x, basis_coeffs, linear_w, pathway_balance, out):

@@ -25,7 +25,6 @@ FLOPS = 2 * R * I * O * (NB + 1)
 
 CRAW_BUFS = 5
 FIRST_SCALAR_HALF = 2
-FORM = 2
 
 
 def tile_kolmogorovarnoldlinear_kernel(tc, x, basis_coeffs, linear_w, pathway_balance, out):
@@ -40,8 +39,10 @@ def tile_kolmogorovarnoldlinear_kernel(tc, x, basis_coeffs, linear_w, pathway_ba
         ctx.enter_context(tc.manual_schedule())
 
         x_sb = keep.tile([P, MT, I], BF16)
-        for m in range(MT):
+
+        def load_x(m):
             nc.sync.dma_start(out=x_sb[:, m, :], in_=xf[m * P:(m + 1) * P, :])
+
         pb_bf = keep.tile([P, 2], BF16)
         nc.scalar.dma_start(out=pb_bf[:], in_=pathway_balance.partition_broadcast(P))
 
@@ -56,7 +57,20 @@ def tile_kolmogorovarnoldlinear_kernel(tc, x, basis_coeffs, linear_w, pathway_ba
             )
             craw[h] = t
 
-        load_half(0)
+        craw[0] = work.tile([P, 4, OC * NB], BF16, name="craw0", tag="craw", bufs=CRAW_BUFS)
+
+        def load_half0(part):
+            nc.sync.dma_start(
+                out=craw[0][:, :, 640 * part:640 * part + 640],
+                in_=basis_coeffs[0:512, 128 * part:128 * part + 128, :].rearrange("(p j) o n -> p j (o n)", j=4),
+            )
+
+        load_x(0)
+        load_half0(0)
+        load_x(1)
+        load_half0(1)
+        load_x(2)
+        load_x(3)
         load_half(1)
         w_sb = keep.tile([P, O // P, I], BF16)
         wv = linear_w.rearrange("(a p) i -> p a i", p=P)
@@ -116,43 +130,14 @@ def tile_kolmogorovarnoldlinear_kernel(tc, x, basis_coeffs, linear_w, pathway_ba
         for i in range(4):
             transpose_w(i)
 
-        for m in range(MT):
-            xg = work.tile([P, 1024], BF16, tag="xg", align_bytes=64)
-            nc.scalar.copy(
-                out=xg[:].bitcast(F32).rearrange("p (q u) -> p q u", u=2),
-                in_=xt[m][:].rearrange("p (u q) -> p q u", u=2),
-            )
-            t32 = work.tile([P, 1024], F32, tag="t32")
-            nc.scalar.activation(
-                out=t32[:].rearrange("p (q u e) -> p q u e", u=2, e=2),
-                in_=xt[m][:].bitcast(BF16).rearrange("p (u q e) -> p q u e", u=2, e=2),
-                func=AF.Tanh,
-            )
-            s32 = work.tile([P, 1024], F32, tag="s32")
-            nc.scalar.activation(out=s32[:], in_=t32[:], func=AF.Square)
-            ain = work.tile([P, 4, 1024], BF16, tag="ain", align_bytes=64)
-            nc.scalar.activation(out=ain[:, 3, :], in_=s32[:], func=AF.Square)
-            nc.vector.quantize_mx(out=xq[:, m, :].bitcast(FP8X4), scales=xs[:, m, :], in_=xg[:])
-            nc.vector.tensor_copy(out=ain[:, 0, :], in_=t32[:])
-            nc.vector.tensor_copy(out=ain[:, 1, :], in_=s32[:])
-            nc.vector.tensor_tensor(out=ain[:, 2, :], in0=s32[:], in1=t32[:], op=ALU.mult)
-            nc.vector.quantize_mx(
-                out=aq[:, m, :].bitcast(FP8X4), scales=as_[:, m, :], in_=ain[:].rearrange("p a c -> p (a c)")
-            )
-            transpose_w(4 + m)
-
         cga = {}
         cgb = {}
         cq = {}
         cs = {}
 
-        def regroup(eng, dst_tile, h, lo, hi, base):
-            if FORM == 1:
-                src = craw[h][:].rearrange("p j (o n) -> p o n j", n=NB)[:, :, lo:hi, :]
-                dst = dst_tile[:, lo - base:hi - base, :, :].rearrange("p n o j -> p o n j")
-            else:
-                src = craw[h][:].rearrange("p j (o n) -> p o j n", n=NB)[:, :, :, lo:hi]
-                dst = dst_tile[:, lo - base:hi - base, :, :].rearrange("p n o j -> p o j n")
+        def regroup(eng, dst_tile, h, lo, hi, base, o0=0, o1=OC):
+            src = craw[h][:].rearrange("p j (o n) -> p o j n", n=NB)[:, o0:o1, :, lo:hi]
+            dst = dst_tile[:, lo - base:hi - base, o0:o1, :].rearrange("p n o j -> p o j n")
             if eng == "scalar":
                 nc.scalar.copy(out=dst, in_=src)
             else:
@@ -203,20 +188,79 @@ def tile_kolmogorovarnoldlinear_kernel(tc, x, basis_coeffs, linear_w, pathway_ba
                         stop=(last and n == powers[-1]),
                     )
 
-        def finish(c):
-            for m in range(MT):
-                nc.vector.scalar_tensor_tensor(
-                    out=y[:, m, OC * c:OC * c + OC],
-                    in0=nacc[c][m][:, 0:OC],
-                    scalar=pb32[:, 0:1],
-                    in1=y[:, m, OC * c:OC * c + OC],
-                    op0=ALU.mult,
-                    op1=ALU.add,
-                )
-                if c == NCH - 1:
-                    nc.sync.dma_start(out=ov[:, m, OC * c:OC * c + OC], in_=y[:, m, OC * c:OC * c + OC])
-            if c < NCH - 1:
-                nc.sync.dma_start(out=ov[:, :, OC * c:OC * c + OC], in_=y[:, :, OC * c:OC * c + OC])
+        xg = {}
+        t32 = {}
+        s32 = {}
+        ain = {}
+
+        def s_copy_x(m):
+            xg[m] = work.tile([P, 1024], BF16, name="xg%d" % m, tag="xg", align_bytes=64)
+            nc.scalar.copy(
+                out=xg[m][:].bitcast(F32).rearrange("p (q u) -> p q u", u=2),
+                in_=xt[m][:].rearrange("p (u q) -> p q u", u=2),
+            )
+
+        def s_tanh(m):
+            t32[m] = work.tile([P, 1024], F32, name="t32_%d" % m, tag="t32")
+            nc.scalar.activation(
+                out=t32[m][:].rearrange("p (q u e) -> p q u e", u=2, e=2),
+                in_=xt[m][:].bitcast(BF16).rearrange("p (u q e) -> p q u e", u=2, e=2),
+                func=AF.Tanh,
+            )
+
+        def s_square(m):
+            s32[m] = work.tile([P, 1024], F32, name="s32_%d" % m, tag="s32")
+            nc.scalar.activation(out=s32[m][:], in_=t32[m][:], func=AF.Square)
+
+        def s_fourth(m):
+            nc.scalar.activation(out=ain[m][:, 3, :], in_=s32[m][:], func=AF.Square)
+
+        def v_quantise_x(m):
+            nc.vector.quantize_mx(out=xq[:, m, :].bitcast(FP8X4), scales=xs[:, m, :], in_=xg[m][:])
+
+        def v_first(m):
+            ain[m] = work.tile([P, 4, 1024], BF16, name="ain%d" % m, tag="ain", align_bytes=64)
+            nc.vector.tensor_copy(out=ain[m][:, 0, :], in_=t32[m][:])
+
+        def v_second_third(m):
+            nc.vector.tensor_copy(out=ain[m][:, 1, :], in_=s32[m][:])
+            nc.vector.tensor_tensor(out=ain[m][:, 2, :], in0=s32[m][:], in1=t32[m][:], op=ALU.mult)
+
+        def v_quantise_powers(m):
+            nc.vector.quantize_mx(
+                out=aq[:, m, :].bitcast(FP8X4), scales=as_[:, m, :], in_=ain[m][:].rearrange("p a c -> p (a c)")
+            )
+
+        cga[0] = work.tile([P, 3, OC, 4], BF16, name="cga0", tag="cga", bufs=4, align_bytes=64)
+        cgb[0] = work.tile([P, 2, OC, 4], BF16, name="cgb0", tag="cgb", bufs=2, align_bytes=64)
+
+        def regroup_half0(part, which):
+            o0, o1 = 128 * part, 128 * part + 128
+            if which == "b":
+                regroup("vector", cgb[0], 0, 3, 5, 3, o0, o1)
+            else:
+                regroup("vector", cga[0], 0, 0, 2, 0, o0, o1)
+                regroup("vector", cga[0], 0, 2, 3, 0, o0, o1)
+
+        s_copy_x(0)
+        s_tanh(0)
+        for m in range(MT):
+            v_quantise_x(m)
+            if m == 0:
+                regroup_half0(0, "b")
+            v_first(m)
+            if m == 0:
+                regroup_half0(0, "a")
+            if m > 0:
+                v_quantise_powers(m - 1)
+            if m + 1 < MT:
+                s_copy_x(m + 1)
+            s_square(m)
+            if m + 1 < MT:
+                s_tanh(m + 1)
+            s_fourth(m)
+            v_second_third(m)
+            transpose_w(4 + m)
 
         wg = {}
         for i in range(8):
@@ -228,9 +272,11 @@ def tile_kolmogorovarnoldlinear_kernel(tc, x, basis_coeffs, linear_w, pathway_ba
                 out=wg32[:, 256 * pair:256 * pair + 256, :],
                 in_=wt[i][:].rearrange("p (u o) -> p o u", u=2),
             )
-            if i == 3:
-                vector_regroups(0)
+            if i == 1:
+                regroup_half0(1, "b")
+                regroup_half0(1, "a")
                 load_half(CRAW_BUFS)
+                v_quantise_powers(MT - 1)
             if i % 2 == 1:
                 hq, g = i // 4, (i // 2) % 2
                 nc.vector.quantize_mx(
@@ -256,32 +302,53 @@ def tile_kolmogorovarnoldlinear_kernel(tc, x, basis_coeffs, linear_w, pathway_ba
                     out=y[:, m, 512 * hf:512 * hf + 512], in_=lacc[:], func=AF.Copy, scale=pb32[:, 1:2]
                 )
 
-        for h in range(NH + 2):
-            if h + 1 < NH:
-                vector_regroups(h + 1)
-                if h + 1 < FIRST_SCALAR_HALF and h + 1 + CRAW_BUFS < NH:
-                    load_half(h + 1 + CRAW_BUFS)
-            if h < NH:
-                c, g = divmod(h, G)
-                if g == 0:
-                    nacc[c] = [psum.tile([P, 512], F32, name="nacc%d_%d" % (c, m), tag="bank") for m in range(MT)]
-                cq[h] = work.tile([P, NB, OC], U32, name="cq%d" % h, tag="cq", bufs=4, align_bytes=64)
-                cs[h] = work.tile([P, NB, OC], U8, name="cs%d" % h, tag="cs", bufs=4, align_bytes=64)
-                if h < FIRST_SCALAR_HALF:
-                    quantise(h, cga[h], 0, 0, 2)
-                    quantise(h, cga[h], 0, 2, 3)
-                    quantise(h, cgb[h], 3, 3, 5)
-                    passes(h, (0, 1, 2), g == 0, False)
-                    passes(h, (3, 4), False, g == G - 1)
-                else:
-                    quantise(h, cgb[h], 3, 3, 5)
-                    quantise(h, cga[h], 0, 0, 2)
-                    quantise(h, cga[h], 0, 2, 3)
-                    passes(h, (3, 4), g == 0, False)
-                    passes(h, (0, 1, 2), False, g == G - 1)
-                    if h + CRAW_BUFS < NH:
-                        load_half(h + CRAW_BUFS)
-                if FIRST_SCALAR_HALF < h + 3 < NH:
-                    regroup_a(h + 3, "scalar")
-            if h >= 3 and h % 2 == 1:
-                finish((h - 3) // 2)
+        def finish_rows(c, rows):
+            for m in rows:
+                nc.vector.scalar_tensor_tensor(
+                    out=y[:, m, OC * c:OC * c + OC],
+                    in0=nacc[c][m][:, 0:OC],
+                    scalar=pb32[:, 0:1],
+                    in1=y[:, m, OC * c:OC * c + OC],
+                    op0=ALU.mult,
+                    op1=ALU.add,
+                )
+                if c == NCH - 1:
+                    nc.sync.dma_start(out=ov[:, m, OC * c:OC * c + OC], in_=y[:, m, OC * c:OC * c + OC])
+            if c < NCH - 1 and rows[-1] == MT - 1:
+                nc.sync.dma_start(out=ov[:, :, OC * c:OC * c + OC], in_=y[:, :, OC * c:OC * c + OC])
+
+        for h in range(NH):
+            c, g = divmod(h, G)
+            done = (h - 3) // 2 if (h >= 3 and h % 2 == 1) else -1
+            if g == 0:
+                nacc[c] = [psum.tile([P, 512], F32, name="nacc%d_%d" % (c, m), tag="bank") for m in range(MT)]
+            cq[h] = work.tile([P, NB, OC], U32, name="cq%d" % h, tag="cq", bufs=4, align_bytes=64)
+            cs[h] = work.tile([P, NB, OC], U8, name="cs%d" % h, tag="cs", bufs=4, align_bytes=64)
+            if h < FIRST_SCALAR_HALF:
+                if h + 1 < NH:
+                    vector_regroups(h + 1)
+                    if h + 1 < FIRST_SCALAR_HALF and h + 1 + CRAW_BUFS < NH:
+                        load_half(h + 1 + CRAW_BUFS)
+                quantise(h, cga[h], 0, 0, 2)
+                quantise(h, cga[h], 0, 2, 3)
+                quantise(h, cgb[h], 3, 3, 5)
+                passes(h, (0, 1, 2), g == 0, False)
+                passes(h, (3, 4), False, g == G - 1)
+            else:
+                quantise(h, cgb[h], 3, 3, 5)
+                passes(h, (3, 4), g == 0, False)
+                if h + 1 < NH:
+                    vector_regroups(h + 1)
+                if done >= 0:
+                    finish_rows(done, (0, 1))
+                quantise(h, cga[h], 0, 0, 2)
+                passes(h, (0, 1), False, False)
+                if done >= 0:
+                    finish_rows(done, (2, 3))
+                quantise(h, cga[h], 0, 2, 3)
+                passes(h, (2,), False, g == G - 1)
+                if h + CRAW_BUFS < NH:
+                    load_half(h + CRAW_BUFS)
+            if FIRST_SCALAR_HALF < h + 3 < NH:
+                regroup_a(h + 3, "scalar")
+        finish_rows(NCH - 1, (0, 1, 2, 3))

@@ -35,7 +35,7 @@ def tile_kolmogorovarnoldlinear_kernel(tc, x, basis_coeffs, linear_w, pathway_ba
     with ExitStack() as ctx:
         keep = ctx.enter_context(tc.tile_pool(name="keep", bufs=1))
         work = ctx.enter_context(tc.tile_pool(name="work", bufs=2))
-        psum = ctx.enter_context(tc.psum_pool(name="psum", bufs=8))
+        psum = ctx.enter_context(tc.psum_pool(name="psum", bufs=4))
         ctx.enter_context(tc.manual_schedule())
 
         x_sb = keep.tile([P, MT, I], BF16)
@@ -103,7 +103,7 @@ def tile_kolmogorovarnoldlinear_kernel(tc, x, basis_coeffs, linear_w, pathway_ba
         wt = {}
 
         def transpose_x(m):
-            xt[m] = psum.tile([P, 512], F32, name="xt%d" % m, tag="bank")
+            xt[m] = psum.tile([P, 512], F32, name="xt%d" % m, tag="pa")
             for u in range(2):
                 for g in range(G):
                     k = 2 * u + g
@@ -115,7 +115,7 @@ def tile_kolmogorovarnoldlinear_kernel(tc, x, basis_coeffs, linear_w, pathway_ba
 
         def transpose_w(i):
             hq, g, pair = i // 4, (i // 2) % 2, i % 2
-            wt[i] = psum.tile([P, 512], F32, name="wt%d" % i, tag="bank")
+            wt[i] = psum.tile([P, 512], F32, name="wt%d" % i, tag="pb")
             for a2 in range(2):
                 a = 4 * hq + 2 * pair + a2
                 for u in range(2):
@@ -169,10 +169,10 @@ def tile_kolmogorovarnoldlinear_kernel(tc, x, basis_coeffs, linear_w, pathway_ba
 
         nacc = {}
 
-        def passes(h, powers, first, last):
+        def passes(h, powers, first, last, rows=(0, 1, 2, 3)):
             c, g = divmod(h, G)
             for n in powers:
-                for m in range(MT):
+                for m in rows:
                     if n == 0:
                         lhsT, lsc = oneq[:], ones_s[:]
                     else:
@@ -260,23 +260,41 @@ def tile_kolmogorovarnoldlinear_kernel(tc, x, basis_coeffs, linear_w, pathway_ba
                 s_tanh(m + 1)
             s_fourth(m)
             v_second_third(m)
-            transpose_w(4 + m)
+
+        def new_half(h):
+            c, g = divmod(h, G)
+            if g == 0:
+                nacc[c] = [
+                    psum.tile([P, 512], F32, name="nacc%d_%d" % (c, m), tag=("pa" if c % 2 == 0 else "pb"))
+                    for m in range(MT)
+                ]
+            cq[h] = work.tile([P, NB, OC], U32, name="cq%d" % h, tag="cq", bufs=4, align_bytes=64)
+            cs[h] = work.tile([P, NB, OC], U8, name="cs%d" % h, tag="cs", bufs=4, align_bytes=64)
 
         wg = {}
         for i in range(8):
             if i % 2 == 0:
-                wg[i // 2] = work.tile([P, 2048], BF16, name="wg%d" % (i // 2), tag="wg", bufs=2, align_bytes=64)
+                wg[i // 2] = work.tile([P, 2048], BF16, name="wg%d" % (i // 2), tag="wg", bufs=3, align_bytes=64)
             wg32 = wg[i // 2][:].bitcast(F32).rearrange("p (o u) -> p o u", u=2)
             pair = i % 2
             nc.scalar.copy(
                 out=wg32[:, 256 * pair:256 * pair + 256, :],
                 in_=wt[i][:].rearrange("p (u o) -> p o u", u=2),
             )
-            if i == 1:
+            if i < 4:
+                transpose_w(4 + i)
+            if i == 3:
                 regroup_half0(1, "b")
                 regroup_half0(1, "a")
                 load_half(CRAW_BUFS)
+                new_half(0)
+                quantise(0, cgb[0], 3, 3, 5)
+                quantise(0, cga[0], 0, 0, 2)
+                quantise(0, cga[0], 0, 2, 3)
+                for m in range(MT - 1):
+                    passes(0, (3, 4, 0, 1, 2), True, False, (m,))
                 v_quantise_powers(MT - 1)
+                passes(0, (3, 4, 0, 1, 2), True, False, (MT - 1,))
             if i % 2 == 1:
                 hq, g = i // 4, (i // 2) % 2
                 nc.vector.quantize_mx(
@@ -287,7 +305,7 @@ def tile_kolmogorovarnoldlinear_kernel(tc, x, basis_coeffs, linear_w, pathway_ba
         regroup_a(FIRST_SCALAR_HALF, "scalar")
         for m in range(MT):
             for hf in range(2):
-                lacc = psum.tile([P, 512], F32, name="lacc%d%d" % (m, hf), tag="bank")
+                lacc = psum.tile([P, 512], F32, name="lacc%d%d" % (m, hf), tag="pb")
                 for g in range(G):
                     nc.tensor.matmul_mx(
                         out=lacc[:],
@@ -320,15 +338,13 @@ def tile_kolmogorovarnoldlinear_kernel(tc, x, basis_coeffs, linear_w, pathway_ba
         for h in range(NH):
             c, g = divmod(h, G)
             done = (h - 3) // 2 if (h >= 3 and h % 2 == 1) else -1
-            if g == 0:
-                nacc[c] = [psum.tile([P, 512], F32, name="nacc%d_%d" % (c, m), tag="bank") for m in range(MT)]
-            cq[h] = work.tile([P, NB, OC], U32, name="cq%d" % h, tag="cq", bufs=4, align_bytes=64)
-            cs[h] = work.tile([P, NB, OC], U8, name="cs%d" % h, tag="cs", bufs=4, align_bytes=64)
-            if h < FIRST_SCALAR_HALF:
-                if h + 1 < NH:
-                    vector_regroups(h + 1)
-                    if h + 1 < FIRST_SCALAR_HALF and h + 1 + CRAW_BUFS < NH:
-                        load_half(h + 1 + CRAW_BUFS)
+            if h > 0:
+                new_half(h)
+            if h == 0:
+                vector_regroups(1)
+                load_half(1 + CRAW_BUFS)
+            elif h < FIRST_SCALAR_HALF:
+                vector_regroups(h + 1)
                 quantise(h, cga[h], 0, 0, 2)
                 quantise(h, cga[h], 0, 2, 3)
                 quantise(h, cgb[h], 3, 3, 5)

@@ -148,8 +148,7 @@ def tile_kolmogorovarnoldlinear_kernel(tc, x, basis_coeffs, linear_w, pathway_ba
             if eng == "scalar":
                 regroup(eng, cga[h], h, 0, 3, 0)
             else:
-                regroup(eng, cga[h], h, 0, 2, 0)
-                regroup(eng, cga[h], h, 2, 3, 0)
+                regroup(eng, cga[h], h, 0, 3, 0)
 
         def regroup_b(h):
             cgb[h] = work.tile([P, 2, OC, 4], BF16, name="cgb%d" % h, tag="cgb", bufs=2, align_bytes=64)
@@ -179,7 +178,7 @@ def tile_kolmogorovarnoldlinear_kernel(tc, x, basis_coeffs, linear_w, pathway_ba
                         k = (n - 1) * G + g
                         lhsT, lsc = aq[:, m, k * P:(k + 1) * P], as_[:, m, k * P:(k + 1) * P]
                     nc.tensor.matmul_mx(
-                        out=nacc[c][m][:, 0:OC],
+                        out=nacc[c][m][:, OC * (c % 2 if c < 2 else 0):OC * (c % 2 if c < 2 else 0) + OC],
                         lhsT=lhsT.bitcast(FP8X4),
                         lhsT_scale=lsc,
                         rhs=cq[h][:, n, :].bitcast(FP8X4),
@@ -239,8 +238,7 @@ def tile_kolmogorovarnoldlinear_kernel(tc, x, basis_coeffs, linear_w, pathway_ba
             if which == "b":
                 regroup("vector", cgb[0], 0, 3, 5, 3, o0, o1)
             else:
-                regroup("vector", cga[0], 0, 0, 2, 0, o0, o1)
-                regroup("vector", cga[0], 0, 2, 3, 0, o0, o1)
+                regroup("vector", cga[0], 0, 0, 3, 0, o0, o1)
 
         s_copy_x(0)
         s_tanh(0)
@@ -263,9 +261,11 @@ def tile_kolmogorovarnoldlinear_kernel(tc, x, basis_coeffs, linear_w, pathway_ba
 
         def new_half(h):
             c, g = divmod(h, G)
-            if g == 0:
+            if g == 0 and c == 1:
+                nacc[c] = nacc[0]
+            elif g == 0:
                 nacc[c] = [
-                    psum.tile([P, 512], F32, name="nacc%d_%d" % (c, m), tag=("pa" if c % 2 == 0 else "pb"))
+                    psum.tile([P, 512], F32, name="nacc%d_%d" % (c, m), tag=("pb" if c == 2 else "pa"))
                     for m in range(MT)
                 ]
             cq[h] = work.tile([P, NB, OC], U32, name="cq%d" % h, tag="cq", bufs=4, align_bytes=64)
@@ -321,19 +321,22 @@ def tile_kolmogorovarnoldlinear_kernel(tc, x, basis_coeffs, linear_w, pathway_ba
                 )
 
         def finish_rows(c, rows):
+            if c == 0:
+                return
+            lo, width = (0, 2 * OC) if c == 1 else (OC * c, OC)
             for m in rows:
                 nc.vector.scalar_tensor_tensor(
-                    out=y[:, m, OC * c:OC * c + OC],
-                    in0=nacc[c][m][:, 0:OC],
+                    out=y[:, m, lo:lo + width],
+                    in0=nacc[c][m][:, 0:width],
                     scalar=pb32[:, 0:1],
-                    in1=y[:, m, OC * c:OC * c + OC],
+                    in1=y[:, m, lo:lo + width],
                     op0=ALU.mult,
                     op1=ALU.add,
                 )
                 if c == NCH - 1:
-                    nc.sync.dma_start(out=ov[:, m, OC * c:OC * c + OC], in_=y[:, m, OC * c:OC * c + OC])
+                    nc.sync.dma_start(out=ov[:, m, lo:lo + width], in_=y[:, m, lo:lo + width])
             if c < NCH - 1 and rows[-1] == MT - 1:
-                nc.sync.dma_start(out=ov[:, :, OC * c:OC * c + OC], in_=y[:, :, OC * c:OC * c + OC])
+                nc.sync.dma_start(out=ov[:, :, lo:lo + width], in_=y[:, :, lo:lo + width])
 
         for h in range(NH):
             c, g = divmod(h, G)

@@ -356,12 +356,12 @@ def tile_kolmogorovarnoldlinear_kernel(tc, x, basis_coeffs, linear_w, pathway_ba
             else:
                 quantise(h, cgb[h], 3, 3, 5)
                 passes(h, (3, 4), g == 0, False)
-                if h + 1 < NH:
-                    vector_regroups(h + 1)
                 if done >= 0:
                     finish_rows(done, (0, 1))
                 quantise(h, cga[h], 0, 0, 2)
                 passes(h, (0, 1), False, False)
+                if h + 1 < NH:
+                    vector_regroups(h + 1)
                 if done >= 0:
                     finish_rows(done, (2, 3))
                 quantise(h, cga[h], 0, 2, 3)

@@ -136,8 +136,8 @@ def tile_kolmogorovarnoldlinear_kernel(tc, x, basis_coeffs, linear_w, pathway_ba
         cs = {}
 
         def regroup(eng, dst_tile, h, lo, hi, base, o0=0, o1=OC):
-            src = craw[h][:].rearrange("p j (o n) -> p o j n", n=NB)[:, o0:o1, :, lo:hi]
-            dst = dst_tile[:, lo - base:hi - base, o0:o1, :].rearrange("p n o j -> p o j n")
+            src = craw[h][:].rearrange("p j (c i n) -> p c j i n", i=2, n=NB)[:, o0 // 2:o1 // 2, :, :, lo:hi]
+            dst = dst_tile[:, lo - base:hi - base, o0:o1, :].rearrange("p n (c i) j -> p c j i n", i=2)
             if eng == "scalar":
                 nc.scalar.copy(out=dst, in_=src)
             else:

@@ -136,8 +136,8 @@ def tile_kolmogorovarnoldlinear_kernel(tc, x, basis_coeffs, linear_w, pathway_ba
         cs = {}
 
         def regroup(eng, dst_tile, h, lo, hi, base, o0=0, o1=OC):
-            src = craw[h][:].rearrange("p j (c i n) -> p c j i n", i=2, n=NB)[:, o0 // 2:o1 // 2, :, :, lo:hi]
-            dst = dst_tile[:, lo - base:hi - base, o0:o1, :].rearrange("p n (c i) j -> p c j i n", i=2)
+            src = craw[h][:].rearrange("p j (c i n) -> p c j n i", i=2, n=NB)[:, o0 // 2:o1 // 2, :, lo:hi, :]
+            dst = dst_tile[:, lo - base:hi - base, o0:o1, :].rearrange("p n (c i) j -> p c j n i", i=2)
             if eng == "scalar":
                 nc.scalar.copy(out=dst, in_=src)
             else:

@@ -44,7 +44,6 @@ def tile_kolmogorovarnoldlinear_kernel(tc, x, basis_coeffs, linear_w, pathway_ba
             nc.sync.dma_start(out=x_sb[:, m, :], in_=xf[m * P:(m + 1) * P, :])
 
         pb_bf = keep.tile([P, 2], BF16)
-        nc.scalar.dma_start(out=pb_bf[:], in_=pathway_balance.partition_broadcast(P))
 
         craw = {}
 
@@ -76,7 +75,9 @@ def tile_kolmogorovarnoldlinear_kernel(tc, x, basis_coeffs, linear_w, pathway_ba
         wv = linear_w.rearrange("(a p) i -> p a i", p=P)
         for q in range(2):
             nc.sync.dma_start(out=w_sb[:, 4 * q:4 * q + 4, :], in_=wv[:, 4 * q:4 * q + 4, :])
-        for h in range(2, CRAW_BUFS):
+        load_half(2)
+        nc.sync.dma_start(out=pb_bf[:], in_=pathway_balance.partition_broadcast(P))
+        for h in range(3, CRAW_BUFS):
             load_half(h)
 
         ident = keep.tile([P, P], F32)
@@ -87,7 +88,6 @@ def tile_kolmogorovarnoldlinear_kernel(tc, x, basis_coeffs, linear_w, pathway_ba
         ones_s = keep.tile([P, P], U8, align_bytes=64)
         nc.vector.quantize_mx(out=oneq[:].bitcast(FP8X4), scales=ones_s[:], in_=ones[:])
         pb32 = keep.tile([P, 2], F32)
-        nc.vector.tensor_copy(out=pb32[:], in_=pb_bf[:])
 
         xw = x_sb[:].bitcast(F32)
         ww = w_sb[:].bitcast(F32)
@@ -303,6 +303,7 @@ def tile_kolmogorovarnoldlinear_kernel(tc, x, basis_coeffs, linear_w, pathway_ba
                     in_=wg[i // 2][:],
                 )
         regroup_a(FIRST_SCALAR_HALF, "scalar")
+        nc.scalar.copy(out=pb32[:], in_=pb_bf[:])
         for m in range(MT):
             for hf in range(2):
                 lacc = psum.tile([P, 512], F32, name="lacc%d%d" % (m, hf), tag="pb")

@@ -58,16 +58,17 @@ def tile_kolmogorovarnoldlinear_kernel(tc, x, basis_coeffs, linear_w, pathway_ba
 
         craw[0] = work.tile([P, 4, OC * NB], BF16, name="craw0", tag="craw", bufs=CRAW_BUFS)
 
-        def load_half0(part):
+        def load_half0(o0, o1):
             nc.sync.dma_start(
-                out=craw[0][:, :, 640 * part:640 * part + 640],
-                in_=basis_coeffs[0:512, 128 * part:128 * part + 128, :].rearrange("(p j) o n -> p j (o n)", j=4),
+                out=craw[0][:, :, NB * o0:NB * o1],
+                in_=basis_coeffs[0:512, o0:o1, :].rearrange("(p j) o n -> p j (o n)", j=4),
             )
 
         load_x(0)
-        load_half0(0)
+        load_half0(0, 64)
         load_x(1)
-        load_half0(1)
+        load_half0(64, 128)
+        load_half0(128, 256)
         load_x(2)
         load_x(3)
         load_half(1)
@@ -233,8 +234,7 @@ def tile_kolmogorovarnoldlinear_kernel(tc, x, basis_coeffs, linear_w, pathway_ba
         cga[0] = work.tile([P, 3, OC, 4], BF16, name="cga0", tag="cga", bufs=4, align_bytes=64)
         cgb[0] = work.tile([P, 2, OC, 4], BF16, name="cgb0", tag="cgb", bufs=2, align_bytes=64)
 
-        def regroup_half0(part, which):
-            o0, o1 = 128 * part, 128 * part + 128
+        def regroup_half0(o0, o1, which):
             if which == "b":
                 regroup("vector", cgb[0], 0, 3, 5, 3, o0, o1)
             else:
@@ -245,10 +245,12 @@ def tile_kolmogorovarnoldlinear_kernel(tc, x, basis_coeffs, linear_w, pathway_ba
         for m in range(MT):
             v_quantise_x(m)
             if m == 0:
-                regroup_half0(0, "b")
+                regroup_half0(0, 64, "b")
+                regroup_half0(0, 64, "a")
             v_first(m)
             if m == 0:
-                regroup_half0(0, "a")
+                regroup_half0(64, 128, "b")
+                regroup_half0(64, 128, "a")
             if m > 0:
                 v_quantise_powers(m - 1)
             if m + 1 < MT:
@@ -271,6 +273,8 @@ def tile_kolmogorovarnoldlinear_kernel(tc, x, basis_coeffs, linear_w, pathway_ba
             cq[h] = work.tile([P, NB, OC], U32, name="cq%d" % h, tag="cq", bufs=4, align_bytes=64)
             cs[h] = work.tile([P, NB, OC], U8, name="cs%d" % h, tag="cs", bufs=4, align_bytes=64)
 
+        regroup_half0(128, 256, "b")
+        regroup_half0(128, 256, "a")
         wg = {}
         for i in range(8):
             if i % 2 == 0:
@@ -284,8 +288,6 @@ def tile_kolmogorovarnoldlinear_kernel(tc, x, basis_coeffs, linear_w, pathway_ba
             if i < 4:
                 transpose_w(4 + i)
             if i == 3:
-                regroup_half0(1, "b")
-                regroup_half0(1, "a")
                 load_half(CRAW_BUFS)
                 new_half(0)
                 quantise(0, cgb[0], 3, 3, 5)
@@ -336,7 +338,11 @@ def tile_kolmogorovarnoldlinear_kernel(tc, x, basis_coeffs, linear_w, pathway_ba
                 )
                 if c == NCH - 1:
                     nc.sync.dma_start(out=ov[:, m, lo:lo + width], in_=y[:, m, lo:lo + width])
-            if c < NCH - 1 and rows[-1] == MT - 1:
+            if c == NCH - 2:
+                nc.sync.dma_start(
+                    out=ov[:, rows[0]:rows[-1] + 1, lo:lo + width], in_=y[:, rows[0]:rows[-1] + 1, lo:lo + width]
+                )
+            if c < NCH - 2 and rows[-1] == MT - 1:
                 nc.sync.dma_start(out=ov[:, :, lo:lo + width], in_=y[:, :, lo:lo + width])
 
         for h in range(NH):
@@ -354,6 +360,15 @@ def tile_kolmogorovarnoldlinear_kernel(tc, x, basis_coeffs, linear_w, pathway_ba
                 quantise(h, cgb[h], 3, 3, 5)
                 passes(h, (0, 1, 2), g == 0, False)
                 passes(h, (3, 4), False, g == G - 1)
+            elif h + 1 == NH:
+                quantise(h, cgb[h], 3, 3, 5)
+                passes(h, (3, 4), False, False)
+                finish_rows(done, (0, 1))
+                quantise(h, cga[h], 0, 0, 2)
+                quantise(h, cga[h], 0, 2, 3)
+                for m in range(MT):
+                    passes(h, (0, 1, 2), False, True, (m,))
+                finish_rows(done, (2, 3))
             else:
                 quantise(h, cgb[h], 3, 3, 5)
                 passes(h, (3, 4), g == 0, False)

@@ -50,19 +50,22 @@ def tile_kolmogorovarnoldlinear_kernel(tc, x, basis_coeffs, linear_w, pathway_ba
         def load_half(h):
             c, g = divmod(h, G)
             t = work.tile([P, 4, OC * NB], BF16, name="craw%d" % h, tag="craw", bufs=CRAW_BUFS)
-            nc.sync.dma_start(
-                out=t[:],
-                in_=basis_coeffs[512 * g:512 * g + 512, OC * c:OC * c + OC, :].rearrange("(p j) o n -> p j (o n)", j=4),
-            )
+            for u in range(2):
+                k0 = 512 * g + 256 * u
+                nc.sync.dma_start(
+                    out=t[:, 2 * u:2 * u + 2, :],
+                    in_=basis_coeffs[k0:k0 + 256, OC * c:OC * c + OC, :].rearrange("(p e) o n -> p e (o n)", e=2),
+                )
             craw[h] = t
 
         craw[0] = work.tile([P, 4, OC * NB], BF16, name="craw0", tag="craw", bufs=CRAW_BUFS)
 
         def load_half0(o0, o1):
-            nc.sync.dma_start(
-                out=craw[0][:, :, NB * o0:NB * o1],
-                in_=basis_coeffs[0:512, o0:o1, :].rearrange("(p j) o n -> p j (o n)", j=4),
-            )
+            for u in range(2):
+                nc.sync.dma_start(
+                    out=craw[0][:, 2 * u:2 * u + 2, NB * o0:NB * o1],
+                    in_=basis_coeffs[256 * u:256 * u + 256, o0:o1, :].rearrange("(p e) o n -> p e (o n)", e=2),
+                )
 
         load_x(0)
         load_half0(0, 64)
@@ -110,7 +113,7 @@ def tile_kolmogorovarnoldlinear_kernel(tc, x, basis_coeffs, linear_w, pathway_ba
                     k = 2 * u + g
                     nc.tensor.transpose(
                         out=xt[m][:, k * P:(k + 1) * P],
-                        in_=xw[:, m, 256 * g + u:256 * g + 256:2],
+                        in_=xw[:, m, 256 * g + 128 * u:256 * g + 128 * u + 128],
                         identity=ident[:],
                     )
 
@@ -122,7 +125,7 @@ def tile_kolmogorovarnoldlinear_kernel(tc, x, basis_coeffs, linear_w, pathway_ba
                 for u in range(2):
                     nc.tensor.transpose(
                         out=wt[i][:, u * 256 + a2 * P:u * 256 + (a2 + 1) * P],
-                        in_=ww[:, a, 256 * g + u:256 * g + 256:2],
+                        in_=ww[:, a, 256 * g + 128 * u:256 * g + 128 * u + 128],
                         identity=ident[:],
                     )
 

from contextlib import ExitStack

import concourse.mybir as mybir
from concourse.masks import make_identity

F32 = mybir.dt.float32
BF16 = mybir.dt.bfloat16
U32 = mybir.dt.uint32
U8 = mybir.dt.uint8
FP8X4 = mybir.dt.float8_e4m3fn_x4
AF = mybir.ActivationFunctionType
ALU = mybir.AluOpType

P = 128
R = 512
I = 1024
O = 1024
NB = 5
MT = R // P
G = I // 512
OC = 256
NCH = O // OC
NH = NCH * G
FLOPS = 2 * R * I * O * (NB + 1)

CRAW_BUFS = 5
FIRST_SCALAR_HALF = 2


def tile_kolmogorovarnoldlinear_kernel(tc, x, basis_coeffs, linear_w, pathway_balance, out):
    nc = tc.nc
    xf = x.flatten_outer_dims()
    of = out.flatten_outer_dims()
    ov = of.rearrange("(m p) o -> p m o", p=P)
    with ExitStack() as ctx:
        keep = ctx.enter_context(tc.tile_pool(name="keep", bufs=1))
        work = ctx.enter_context(tc.tile_pool(name="work", bufs=2))
        psum = ctx.enter_context(tc.psum_pool(name="psum", bufs=4))
        ctx.enter_context(tc.manual_schedule())

        x_sb = keep.tile([P, MT, I], BF16)

        def load_x(m):
            nc.sync.dma_start(out=x_sb[:, m, :], in_=xf[m * P:(m + 1) * P, :])

        pb_bf = keep.tile([P, 2], BF16)

        craw = {}

        def load_half(h):
            c, g = divmod(h, G)
            t = work.tile([P, 4, OC * NB], BF16, name="craw%d" % h, tag="craw", bufs=CRAW_BUFS)
            for u in range(2):
                k0 = 512 * g + 256 * u
                nc.sync.dma_start(
                    out=t[:, 2 * u:2 * u + 2, :],
                    in_=basis_coeffs[k0:k0 + 256, OC * c:OC * c + OC, :].rearrange("(p e) o n -> p e (o n)", e=2),
                )
            craw[h] = t

        craw[0] = work.tile([P, 4, OC * NB], BF16, name="craw0", tag="craw", bufs=CRAW_BUFS)

        def load_half0(o0, o1):
            for u in range(2):
                nc.sync.dma_start(
                    out=craw[0][:, 2 * u:2 * u + 2, NB * o0:NB * o1],
                    in_=basis_coeffs[256 * u:256 * u + 256, o0:o1, :].rearrange("(p e) o n -> p e (o n)", e=2),
                )

        load_x(0)
        load_half0(0, 64)
        load_x(1)
        load_half0(64, 128)
        load_half0(128, 256)
        load_x(2)
        load_x(3)
        load_half(1)
        w_sb = keep.tile([P, O // P, I], BF16)
        wv = linear_w.rearrange("(a p) i -> p a i", p=P)
        for q in range(2):
            nc.sync.dma_start(out=w_sb[:, 4 * q:4 * q + 4, :], in_=wv[:, 4 * q:4 * q + 4, :])
        load_half(2)
        nc.sync.dma_start(out=pb_bf[:], in_=pathway_balance.partition_broadcast(P))
        for h in range(3, CRAW_BUFS):
            load_half(h)

        ident = keep.tile([P, P], F32)
        make_identity(nc, ident[:])
        ones = keep.tile([P, 512], BF16, align_bytes=64)
        nc.vector.memset(ones[:], 1.0)
        oneq = keep.tile([P, P], U32, align_bytes=64)
        ones_s = keep.tile([P, P], U8, align_bytes=64)
        nc.vector.quantize_mx(out=oneq[:].bitcast(FP8X4), scales=ones_s[:], in_=ones[:])
        pb32 = keep.tile([P, 2], F32)

        xw = x_sb[:].bitcast(F32)
        ww = w_sb[:].bitcast(F32)
        xq = keep.tile([P, MT, 256], U32, align_bytes=64)
        xs = keep.tile([P, MT, 256], U8, align_bytes=64)
        aq = keep.tile([P, MT, 1024], U32, align_bytes=64)
        as_ = keep.tile([P, MT, 1024], U8, align_bytes=64)
        wq = keep.tile([P, G, O], U32, align_bytes=64)
        ws = keep.tile([P, G, O], U8, align_bytes=64)
        y = keep.tile([P, MT, O], F32)

        xt = {}
        wt = {}

        def transpose_x(m):
            xt[m] = psum.tile([P, 512], F32, name="xt%d" % m, tag="pa")
            for u in range(2):
                for g in range(G):
                    k = 2 * u + g
                    nc.tensor.transpose(
                        out=xt[m][:, k * P:(k + 1) * P],
                        in_=xw[:, m, 256 * g + 128 * u:256 * g + 128 * u + 128],
                        identity=ident[:],
                    )

        def transpose_w(i):
            hq, g, pair = i // 4, (i // 2) % 2, i % 2
            wt[i] = psum.tile([P, 512], F32, name="wt%d" % i, tag="pb")
            for a2 in range(2):
                a = 4 * hq + 2 * pair + a2
                for u in range(2):
                    nc.tensor.transpose(
                        out=wt[i][:, u * 256 + a2 * P:u * 256 + (a2 + 1) * P],
                        in_=ww[:, a, 256 * g + 128 * u:256 * g + 128 * u + 128],
                        identity=ident[:],
                    )

        for m in range(MT):
            transpose_x(m)
        for i in range(4):
            transpose_w(i)

        cga = {}
        cgb = {}
        cq = {}
        cs = {}

        def regroup(eng, dst_tile, h, lo, hi, base, o0=0, o1=OC):
            src = craw[h][:].rearrange("p j (c i n) -> p c j n i", i=2, n=NB)[:, o0 // 2:o1 // 2, :, lo:hi, :]
            dst = dst_tile[:, lo - base:hi - base, o0:o1, :].rearrange("p n (c i) j -> p c j n i", i=2)
            if eng == "scalar":
                nc.scalar.copy(out=dst, in_=src)
            else:
                nc.vector.tensor_copy(out=dst, in_=src)

        def regroup_a(h, eng):
            cga[h] = work.tile([P, 3, OC, 4], BF16, name="cga%d" % h, tag="cga", bufs=4, align_bytes=64)
            if eng == "scalar":
                regroup(eng, cga[h], h, 0, 3, 0)
            else:
                regroup(eng, cga[h], h, 0, 3, 0)

        def regroup_b(h):
            cgb[h] = work.tile([P, 2, OC, 4], BF16, name="cgb%d" % h, tag="cgb", bufs=2, align_bytes=64)
            regroup("vector", cgb[h], h, 3, 5, 3)

        def vector_regroups(h):
            if h < FIRST_SCALAR_HALF:
                regroup_a(h, "vector")
            regroup_b(h)

        def quantise(h, cg, base, lo, hi):
            nc.vector.quantize_mx(
                out=cq[h][:, lo:hi, :].rearrange("p n o -> p (n o)").bitcast(FP8X4),
                scales=cs[h][:, lo:hi, :].rearrange("p n o -> p (n o)"),
                in_=cg[:, lo - base:hi - base, :, :].rearrange("p n o j -> p (n o j)"),
            )

        nacc = {}

        def passes(h, powers, first, last, rows=(0, 1, 2, 3)):
            c, g = divmod(h, G)
            for n in powers:
                for m in rows:
                    if n == 0:
                        lhsT, lsc = oneq[:], ones_s[:]
                    else:
                        k = (n - 1) * G + g
                        lhsT, lsc = aq[:, m, k * P:(k + 1) * P], as_[:, m, k * P:(k + 1) * P]
                    nc.tensor.matmul_mx(
                        out=nacc[c][m][:, OC * (c % 2 if c < 2 else 0):OC * (c % 2 if c < 2 else 0) + OC],
                        lhsT=lhsT.bitcast(FP8X4),
                        lhsT_scale=lsc,
                        rhs=cq[h][:, n, :].bitcast(FP8X4),
                        rhs_scale=cs[h][:, n, :],
                        start=(first and n == powers[0]),
                        stop=(last and n == powers[-1]),
                    )

        xg = {}
        t32 = {}
        s32 = {}
        ain = {}

        def s_copy_x(m):
            xg[m] = work.tile([P, 1024], BF16, name="xg%d" % m, tag="xg", align_bytes=64)
            nc.scalar.copy(
                out=xg[m][:].bitcast(F32).rearrange("p (q u) -> p q u", u=2),
                in_=xt[m][:].rearrange("p (u q) -> p q u", u=2),
            )

        def s_tanh(m):
            t32[m] = work.tile([P, 1024], F32, name="t32_%d" % m, tag="t32")
            nc.scalar.activation(
                out=t32[m][:].rearrange("p (q u e) -> p q u e", u=2, e=2),
                in_=xt[m][:].bitcast(BF16).rearrange("p (u q e) -> p q u e", u=2, e=2),
                func=AF.Tanh,
            )

        def s_square(m):
            s32[m] = work.tile([P, 1024], F32, name="s32_%d" % m, tag="s32")
            nc.scalar.activation(out=s32[m][:], in_=t32[m][:], func=AF.Square)

        def s_fourth(m):
            nc.scalar.activation(out=ain[m][:, 3, :], in_=s32[m][:], func=AF.Square)

        def v_quantise_x(m):
            nc.vector.quantize_mx(out=xq[:, m, :].bitcast(FP8X4), scales=xs[:, m, :], in_=xg[m][:])

        def v_first(m):
            ain[m] = work.tile([P, 4, 1024], BF16, name="ain%d" % m, tag="ain", align_bytes=64)
            nc.vector.tensor_copy(out=ain[m][:, 0, :], in_=t32[m][:])

        def v_second_third(m):
            nc.vector.tensor_copy(out=ain[m][:, 1, :], in_=s32[m][:])
            nc.vector.tensor_tensor(out=ain[m][:, 2, :], in0=s32[m][:], in1=t32[m][:], op=ALU.mult)

        def v_quantise_powers(m):
            nc.vector.quantize_mx(
                out=aq[:, m, :].bitcast(FP8X4), scales=as_[:, m, :], in_=ain[m][:].rearrange("p a c -> p (a c)")
            )

        cga[0] = work.tile([P, 3, OC, 4], BF16, name="cga0", tag="cga", bufs=4, align_bytes=64)
        cgb[0] = work.tile([P, 2, OC, 4], BF16, name="cgb0", tag="cgb", bufs=2, align_bytes=64)

        def regroup_half0(o0, o1, which):
            if which == "b":
                regroup("vector", cgb[0], 0, 3, 5, 3, o0, o1)
            else:
                regroup("vector", cga[0], 0, 0, 3, 0, o0, o1)

        s_copy_x(0)
        s_tanh(0)
        for m in range(MT):
            v_quantise_x(m)
            if m == 0:
                regroup_half0(0, 64, "b")
                regroup_half0(0, 64, "a")
            v_first(m)
            if m == 0:
                regroup_half0(64, 128, "b")
                regroup_half0(64, 128, "a")
            if m > 0:
                v_quantise_powers(m - 1)
            if m + 1 < MT:
                s_copy_x(m + 1)
            s_square(m)
            if m + 1 < MT:
                s_tanh(m + 1)
            s_fourth(m)
            v_second_third(m)

        def new_half(h):
            c, g = divmod(h, G)
            if g == 0 and c == 1:
                nacc[c] = nacc[0]
            elif g == 0:
                nacc[c] = [
                    psum.tile([P, 512], F32, name="nacc%d_%d" % (c, m), tag=("pb" if c == 2 else "pa"))
                    for m in range(MT)
                ]
            cq[h] = work.tile([P, NB, OC], U32, name="cq%d" % h, tag="cq", bufs=4, align_bytes=64)
            cs[h] = work.tile([P, NB, OC], U8, name="cs%d" % h, tag="cs", bufs=4, align_bytes=64)

        regroup_half0(128, 256, "b")
        regroup_half0(128, 256, "a")
        wg = {}
        for i in range(8):
            if i % 2 == 0:
                wg[i // 2] = work.tile([P, 2048], BF16, name="wg%d" % (i // 2), tag="wg", bufs=3, align_bytes=64)
            wg32 = wg[i // 2][:].bitcast(F32).rearrange("p (o u) -> p o u", u=2)
            pair = i % 2
            nc.scalar.copy(
                out=wg32[:, 256 * pair:256 * pair + 256, :],
                in_=wt[i][:].rearrange("p (u o) -> p o u", u=2),
            )
            if i < 4:
                transpose_w(4 + i)
            if i == 3:
                load_half(CRAW_BUFS)
                new_half(0)
                quantise(0, cgb[0], 3, 3, 5)
                quantise(0, cga[0], 0, 0, 2)
                quantise(0, cga[0], 0, 2, 3)
                for m in range(MT - 1):
                    passes(0, (3, 4, 0, 1, 2), True, False, (m,))
                v_quantise_powers(MT - 1)
                passes(0, (3, 4, 0, 1, 2), True, False, (MT - 1,))
            if i % 2 == 1:
                hq, g = i // 4, (i // 2) % 2
                nc.vector.quantize_mx(
                    out=wq[:, g, 512 * hq:512 * hq + 512].bitcast(FP8X4),
                    scales=ws[:, g, 512 * hq:512 * hq + 512],
                    in_=wg[i // 2][:],
                )
        regroup_a(FIRST_SCALAR_HALF, "scalar")
        nc.scalar.copy(out=pb32[:], in_=pb_bf[:])
        for m in range(MT):
            for hf in range(2):
                lacc = psum.tile([P, 512], F32, name="lacc%d%d" % (m, hf), tag="pb")
                for g in range(G):
                    nc.tensor.matmul_mx(
                        out=lacc[:],
                        lhsT=xq[:, m, g * P:(g + 1) * P].bitcast(FP8X4),
                        lhsT_scale=xs[:, m, g * P:(g + 1) * P],
                        rhs=wq[:, g, 512 * hf:512 * hf + 512].bitcast(FP8X4),
                        rhs_scale=ws[:, g, 512 * hf:512 * hf + 512],
                        start=(g == 0),
                        stop=(g == G - 1),
                    )
                nc.scalar.activation(
                    out=y[:, m, 512 * hf:512 * hf + 512], in_=lacc[:], func=AF.Copy, scale=pb32[:, 1:2]
                )

        def finish_rows(c, rows):
            if c == 0:
                return
            lo, width = (0, 2 * OC) if c == 1 else (OC * c, OC)
            for m in rows:
                nc.vector.scalar_tensor_tensor(
                    out=y[:, m, lo:lo + width],
                    in0=nacc[c][m][:, 0:width],
                    scalar=pb32[:, 0:1],
                    in1=y[:, m, lo:lo + width],
                    op0=ALU.mult,
                    op1=ALU.add,
                )
                if c == NCH - 1:
                    nc.sync.dma_start(out=ov[:, m, lo:lo + width], in_=y[:, m, lo:lo + width])
            if c == NCH - 2:
                nc.sync.dma_start(
                    out=ov[:, rows[0]:rows[-1] + 1, lo:lo + width], in_=y[:, rows[0]:rows[-1] + 1, lo:lo + width]
                )
            if c < NCH - 2 and rows[-1] == MT - 1:
                nc.sync.dma_start(out=ov[:, :, lo:lo + width], in_=y[:, :, lo:lo + width])

        for h in range(NH):
            c, g = divmod(h, G)
            done = (h - 3) // 2 if (h >= 3 and h % 2 == 1) else -1
            if h > 0:
                new_half(h)
            if h == 0:
                vector_regroups(1)
                load_half(1 + CRAW_BUFS)
            elif h < FIRST_SCALAR_HALF:
                vector_regroups(h + 1)
                quantise(h, cga[h], 0, 0, 2)
                quantise(h, cga[h], 0, 2, 3)
                quantise(h, cgb[h], 3, 3, 5)
                passes(h, (0, 1, 2), g == 0, False)
                passes(h, (3, 4), False, g == G - 1)
            elif h + 1 == NH:
                quantise(h, cgb[h], 3, 3, 5)
                passes(h, (3, 4), False, False)
                finish_rows(done, (0, 1))
                quantise(h, cga[h], 0, 0, 2)
                quantise(h, cga[h], 0, 2, 3)
                for m in range(MT):
                    passes(h, (0, 1, 2), False, True, (m,))
                finish_rows(done, (2, 3))
            else:
                quantise(h, cgb[h], 3, 3, 5)
                passes(h, (3, 4), g == 0, False)
                if done >= 0:
                    finish_rows(done, (0, 1))
                quantise(h, cga[h], 0, 0, 2)
                passes(h, (0, 1), False, False)
                if h + 1 < NH:
                    vector_regroups(h + 1)
                if done >= 0:
                    finish_rows(done, (2, 3))
                quantise(h, cga[h], 0, 2, 3)
                passes(h, (2,), False, g == G - 1)
                if h + CRAW_BUFS < NH:
                    load_half(h + CRAW_BUFS)
            if FIRST_SCALAR_HALF < h + 3 < NH:
                regroup_a(h + 3, "scalar")
        finish_rows(NCH - 1, (0, 1, 2, 3))
